import numpy as np
import ml_dtypes

BF16 = ml_dtypes.bfloat16


def bf(x):
    return np.asarray(x, np.float32).astype(BF16)


def f32(x):
    return np.asarray(x, np.float32)


def f64(x):
    return np.asarray(x).astype(np.float64)


def striped(idx):
    return np.tile(idx.reshape(-1, 16).T, (8, 1))


C, S, N = 1024, 512, 256


def setup_inputs():
    return {"base": f32(np.random.standard_normal((C, S))), "own_vals": f32(np.random.standard_normal((C, N))), "poi_vals": f32(np.random.standard_normal((C, N))), "offs": striped(np.random.permutation(S)[:N])}


def reference(base, own_vals, poi_vals, offs):
    idx = offs[:16].T.reshape(-1)
    res = f64(base).copy()
    res[:, idx] = f64(own_vals) + f64(poi_vals)
    return res

@@ -1,0 +1,34 @@
+import concourse.mybir as mybir
+
+F32, U16 = mybir.dt.float32, mybir.dt.uint16
+ADD = mybir.AluOpType.add
+P = 128
+
+
+def tile_auxcmp_kernel(tc, base, own_vals, poi_vals, offs, out):
+    nc = tc.nc
+    channels, cells = base.shape
+    listed = own_vals.shape[1]
+    blocks = channels // P
+
+    base_blocks = base.rearrange("(b p) s -> b p s", p=P)
+    own_blocks = own_vals.rearrange("(b p) n -> b p n", p=P)
+    poi_blocks = poi_vals.rearrange("(b p) n -> b p n", p=P)
+    out_blocks = out.rearrange("(b p) s -> b p s", p=P)
+
+    with (
+        tc.tile_pool(name="held", bufs=1) as held,
+        tc.tile_pool(name="work", bufs=blocks) as work,
+    ):
+        offsets = held.tile([P, listed // 16], U16, name="offsets")
+        nc.sync.dma_start(offsets[:], offs)
+
+        for b in range(blocks):
+            window = work.tile([P, cells], F32, name="window")
+            own = work.tile([P, listed], F32, name="own")
+            poi = work.tile([P, listed], F32, name="poi")
+            nc.sync.dma_start(window[:], base_blocks[b])
+            nc.scalar.dma_start(own[:], own_blocks[b])
+            nc.scalar.dma_start(poi[:], poi_blocks[b])
+            nc.vector.tensor_tensor(window[:].indirect(offsets[:]), own[:], poi[:], ADD)
+            nc.gpsimd.dma_start(out_blocks[b], window[:])

@@ -23,6 +23,7 @@ def tile_auxcmp_kernel(tc, base, own_vals, poi_vals, offs, out):
         offsets = held.tile([P, listed // 16], U16, name="offsets")
         nc.sync.dma_start(offsets[:], offs)
 
+        windows, owns, pois = [], [], []
         for b in range(blocks):
             window = work.tile([P, cells], F32, name="window")
             own = work.tile([P, listed], F32, name="own")
@@ -30,5 +31,10 @@ def tile_auxcmp_kernel(tc, base, own_vals, poi_vals, offs, out):
             nc.sync.dma_start(window[:], base_blocks[b])
             nc.scalar.dma_start(own[:], own_blocks[b])
             nc.scalar.dma_start(poi[:], poi_blocks[b])
-            nc.vector.tensor_tensor(window[:].indirect(offsets[:]), own[:], poi[:], ADD)
-            nc.gpsimd.dma_start(out_blocks[b], window[:])
+            windows.append(window)
+            owns.append(own)
+            pois.append(poi)
+
+        for b in range(blocks):
+            nc.vector.tensor_tensor(windows[b][:].indirect(offsets[:]), owns[b][:], pois[b][:], ADD)
+            nc.sync.dma_start(out_blocks[b], windows[b][:])

@@ -11,30 +11,35 @@ def tile_auxcmp_kernel(tc, base, own_vals, poi_vals, offs, out):
     listed = own_vals.shape[1]
     blocks = channels // P
 
-    base_blocks = base.rearrange("(b p) s -> b p s", p=P)
-    own_blocks = own_vals.rearrange("(b p) n -> b p n", p=P)
-    poi_blocks = poi_vals.rearrange("(b p) n -> b p n", p=P)
-    out_blocks = out.rearrange("(b p) s -> b p s", p=P)
+    base_blocks = base.rearrange("(p b) s -> b p s", b=blocks)
+    out_blocks = out.rearrange("(p b) s -> b p s", b=blocks)
+    own_rows = own_vals.rearrange("(p b) n -> p (b n)", b=blocks)
+    poi_rows = poi_vals.rearrange("(p b) n -> p (b n)", b=blocks)
 
-    with (
-        tc.tile_pool(name="held", bufs=1) as held,
-        tc.tile_pool(name="work", bufs=blocks) as work,
-    ):
+    group_starts = [0] + [2**k for k in range(blocks.bit_length() - 1)]
+
+    with tc.tile_pool(name="held", bufs=1) as held:
         offsets = held.tile([P, listed // 16], U16, name="offsets")
         nc.sync.dma_start(offsets[:], offs)
 
-        windows, owns, pois = [], [], []
+        windows = []
         for b in range(blocks):
-            window = work.tile([P, cells], F32, name="window")
-            own = work.tile([P, listed], F32, name="own")
-            poi = work.tile([P, listed], F32, name="poi")
+            window = held.tile([P, cells], F32, name=f"window{b}")
             nc.sync.dma_start(window[:], base_blocks[b])
-            nc.scalar.dma_start(own[:], own_blocks[b])
-            nc.scalar.dma_start(poi[:], poi_blocks[b])
             windows.append(window)
-            owns.append(own)
-            pois.append(poi)
+
+        own_of_block, poi_of_block = [], []
+        for first in group_starts:
+            count = max(first, 1)
+            columns = slice(first * listed, (first + count) * listed)
+            own = held.tile([P, count * listed], F32, name=f"own{first}")
+            poi = held.tile([P, count * listed], F32, name=f"poi{first}")
+            nc.scalar.dma_start(own[:], own_rows[:, columns])
+            nc.scalar.dma_start(poi[:], poi_rows[:, columns])
+            for i in range(count):
+                own_of_block.append(own[:, i * listed : (i + 1) * listed])
+                poi_of_block.append(poi[:, i * listed : (i + 1) * listed])
 
         for b in range(blocks):
-            nc.vector.tensor_tensor(windows[b][:].indirect(offsets[:]), owns[b][:], pois[b][:], ADD)
+            nc.vector.tensor_tensor(windows[b][:].indirect(offsets[:]), own_of_block[b], poi_of_block[b], ADD)
             nc.sync.dma_start(out_blocks[b], windows[b][:])

@@ -16,29 +16,30 @@ def tile_auxcmp_kernel(tc, base, own_vals, poi_vals, offs, out):
     own_rows = own_vals.rearrange("(p b) n -> p (b n)", b=blocks)
     poi_rows = poi_vals.rearrange("(p b) n -> p (b n)", b=blocks)
 
-    group_starts = [0] + [2**k for k in range(blocks.bit_length() - 1)]
+    own_loads = {0: 1}
+    own_loads.update({first: min(2, blocks - first) for first in range(1, blocks, 2)})
+    poi_loads = {0: 1, 1: 1}
+    poi_loads.update({first: 2 for first in range(2, blocks, 2)})
 
     with tc.tile_pool(name="held", bufs=1) as held:
         offsets = held.tile([P, listed // 16], U16, name="offsets")
         nc.sync.dma_start(offsets[:], offs)
 
-        windows = []
+        windows, own_of_block, poi_of_block = [], [], []
         for b in range(blocks):
             window = held.tile([P, cells], F32, name=f"window{b}")
             nc.sync.dma_start(window[:], base_blocks[b])
             windows.append(window)
-
-        own_of_block, poi_of_block = [], []
-        for first in group_starts:
-            count = max(first, 1)
-            columns = slice(first * listed, (first + count) * listed)
-            own = held.tile([P, count * listed], F32, name=f"own{first}")
-            poi = held.tile([P, count * listed], F32, name=f"poi{first}")
-            nc.scalar.dma_start(own[:], own_rows[:, columns])
-            nc.scalar.dma_start(poi[:], poi_rows[:, columns])
-            for i in range(count):
-                own_of_block.append(own[:, i * listed : (i + 1) * listed])
-                poi_of_block.append(poi[:, i * listed : (i + 1) * listed])
+            for name, rows, loads, of_block in (
+                ("own", own_rows, own_loads, own_of_block),
+                ("poi", poi_rows, poi_loads, poi_of_block),
+            ):
+                count = loads.get(b, 0)
+                if count:
+                    values = held.tile([P, count * listed], F32, name=f"{name}{b}")
+                    nc.scalar.dma_start(values[:], rows[:, b * listed : (b + count) * listed])
+                    for i in range(count):
+                        of_block.append(values[:, i * listed : (i + 1) * listed])
 
         for b in range(blocks):
             nc.vector.tensor_tensor(windows[b][:].indirect(offsets[:]), own_of_block[b], poi_of_block[b], ADD)

@@ -37,7 +37,7 @@ def tile_auxcmp_kernel(tc, base, own_vals, poi_vals, offs, out):
                 count = loads.get(b, 0)
                 if count:
                     values = held.tile([P, count * listed], F32, name=f"{name}{b}")
-                    nc.scalar.dma_start(values[:], rows[:, b * listed : (b + count) * listed])
+                    nc.sync.dma_start(values[:], rows[:, b * listed : (b + count) * listed])
                     for i in range(count):
                         of_block.append(values[:, i * listed : (i + 1) * listed])
 

@@ -16,10 +16,11 @@ def tile_auxcmp_kernel(tc, base, own_vals, poi_vals, offs, out):
     own_rows = own_vals.rearrange("(p b) n -> p (b n)", b=blocks)
     poi_rows = poi_vals.rearrange("(p b) n -> p (b n)", b=blocks)
 
-    own_loads = {0: 1}
-    own_loads.update({first: min(2, blocks - first) for first in range(1, blocks, 2)})
-    poi_loads = {0: 1, 1: 1}
-    poi_loads.update({first: 2 for first in range(2, blocks, 2)})
+    singly = 3
+    own_loads = {b: 1 for b in range(singly)}
+    own_loads.update({first: min(2, blocks - first) for first in range(singly, blocks, 2)})
+    poi_loads = {b: 1 for b in range(singly + 1)}
+    poi_loads.update({first: 2 for first in range(singly + 1, blocks, 2)})
 
     with tc.tile_pool(name="held", bufs=1) as held:
         offsets = held.tile([P, listed // 16], U16, name="offsets")

@@ -3,6 +3,7 @@ import concourse.mybir as mybir
 F32, U16 = mybir.dt.float32, mybir.dt.uint16
 ADD = mybir.AluOpType.add
 P = 128
+ALIGN = 256
 
 
 def tile_auxcmp_kernel(tc, base, own_vals, poi_vals, offs, out):
@@ -28,7 +29,7 @@ def tile_auxcmp_kernel(tc, base, own_vals, poi_vals, offs, out):
 
         windows, own_of_block, poi_of_block = [], [], []
         for b in range(blocks):
-            window = held.tile([P, cells], F32, name=f"window{b}")
+            window = held.tile([P, cells], F32, name=f"window{b}", align_bytes=ALIGN)
             nc.sync.dma_start(window[:], base_blocks[b])
             windows.append(window)
             for name, rows, loads, of_block in (
@@ -37,7 +38,7 @@ def tile_auxcmp_kernel(tc, base, own_vals, poi_vals, offs, out):
             ):
                 count = loads.get(b, 0)
                 if count:
-                    values = held.tile([P, count * listed], F32, name=f"{name}{b}")
+                    values = held.tile([P, count * listed], F32, name=f"{name}{b}", align_bytes=ALIGN)
                     nc.sync.dma_start(values[:], rows[:, b * listed : (b + count) * listed])
                     for i in range(count):
                         of_block.append(values[:, i * listed : (i + 1) * listed])

@@ -17,11 +17,9 @@ def tile_auxcmp_kernel(tc, base, own_vals, poi_vals, offs, out):
     own_rows = own_vals.rearrange("(p b) n -> p (b n)", b=blocks)
     poi_rows = poi_vals.rearrange("(p b) n -> p (b n)", b=blocks)
 
-    singly = 3
-    own_loads = {b: 1 for b in range(singly)}
-    own_loads.update({first: min(2, blocks - first) for first in range(singly, blocks, 2)})
-    poi_loads = {b: 1 for b in range(singly + 1)}
-    poi_loads.update({first: 2 for first in range(singly + 1, blocks, 2)})
+    own_loads = {0: 1, 1: 1, 2: 2, 4: 4}
+    poi_loads = {0: 1, 1: 2, 3: 5}
+    assert (1 + blocks + len(own_loads) + len(poi_loads) + blocks) % 8 == 0
 
     with tc.tile_pool(name="held", bufs=1) as held:
         offsets = held.tile([P, listed // 16], U16, name="offsets")

@@ -23,7 +23,6 @@ def tile_auxcmp_kernel(tc, base, own_vals, poi_vals, offs, out):
 
     with tc.tile_pool(name="held", bufs=1) as held:
         offsets = held.tile([P, listed // 16], U16, name="offsets")
-        nc.sync.dma_start(offsets[:], offs)
 
         windows, own_of_block, poi_of_block = [], [], []
         for b in range(blocks):
@@ -40,6 +39,8 @@ def tile_auxcmp_kernel(tc, base, own_vals, poi_vals, offs, out):
                     nc.sync.dma_start(values[:], rows[:, b * listed : (b + count) * listed])
                     for i in range(count):
                         of_block.append(values[:, i * listed : (i + 1) * listed])
+            if b == 0:
+                nc.sync.dma_start(offsets[:], offs)
 
         for b in range(blocks):
             nc.vector.tensor_tensor(windows[b][:].indirect(offsets[:]), own_of_block[b], poi_of_block[b], ADD)

@@ -12,10 +12,10 @@ def tile_auxcmp_kernel(tc, base, own_vals, poi_vals, offs, out):
     listed = own_vals.shape[1]
     blocks = channels // P
 
-    base_blocks = base.rearrange("(p b) s -> b p s", b=blocks)
-    out_blocks = out.rearrange("(p b) s -> b p s", b=blocks)
-    own_rows = own_vals.rearrange("(p b) n -> p (b n)", b=blocks)
-    poi_rows = poi_vals.rearrange("(p b) n -> p (b n)", b=blocks)
+    base_blocks = base.rearrange("(b p) s -> b p s", b=blocks)
+    out_blocks = out.rearrange("(b p) s -> b p s", b=blocks)
+    own_rows = own_vals.rearrange("(b p) n -> p b n", b=blocks)
+    poi_rows = poi_vals.rearrange("(b p) n -> p b n", b=blocks)
 
     own_loads = {0: 1, 1: 1, 2: 2, 4: 4}
     poi_loads = {0: 1, 1: 2, 3: 5}
@@ -35,10 +35,10 @@ def tile_auxcmp_kernel(tc, base, own_vals, poi_vals, offs, out):
             ):
                 count = loads.get(b, 0)
                 if count:
-                    values = held.tile([P, count * listed], F32, name=f"{name}{b}", align_bytes=ALIGN)
-                    nc.sync.dma_start(values[:], rows[:, b * listed : (b + count) * listed])
+                    values = held.tile([P, count, listed], F32, name=f"{name}{b}", align_bytes=ALIGN)
+                    nc.sync.dma_start(values[:], rows[:, b : b + count, :])
                     for i in range(count):
-                        of_block.append(values[:, i * listed : (i + 1) * listed])
+                        of_block.append(values[:, i, :])
             if b == 0:
                 nc.sync.dma_start(offsets[:], offs)
 

import concourse.mybir as mybir

F32, U16 = mybir.dt.float32, mybir.dt.uint16
ADD = mybir.AluOpType.add
P = 128
ALIGN = 256


def tile_auxcmp_kernel(tc, base, own_vals, poi_vals, offs, out):
    nc = tc.nc
    channels, cells = base.shape
    listed = own_vals.shape[1]
    blocks = channels // P

    base_blocks = base.rearrange("(b p) s -> b p s", b=blocks)
    out_blocks = out.rearrange("(b p) s -> b p s", b=blocks)
    own_rows = own_vals.rearrange("(b p) n -> p b n", b=blocks)
    poi_rows = poi_vals.rearrange("(b p) n -> p b n", b=blocks)

    own_loads = {0: 1, 1: 1, 2: 2, 4: 4}
    poi_loads = {0: 1, 1: 2, 3: 5}
    assert (1 + blocks + len(own_loads) + len(poi_loads) + blocks) % 8 == 0

    with tc.tile_pool(name="held", bufs=1) as held:
        offsets = held.tile([P, listed // 16], U16, name="offsets")

        windows, own_of_block, poi_of_block = [], [], []
        for b in range(blocks):
            window = held.tile([P, cells], F32, name=f"window{b}", align_bytes=ALIGN)
            nc.sync.dma_start(window[:], base_blocks[b])
            windows.append(window)
            for name, rows, loads, of_block in (
                ("own", own_rows, own_loads, own_of_block),
                ("poi", poi_rows, poi_loads, poi_of_block),
            ):
                count = loads.get(b, 0)
                if count:
                    values = held.tile([P, count, listed], F32, name=f"{name}{b}", align_bytes=ALIGN)
                    nc.sync.dma_start(values[:], rows[:, b : b + count, :])
                    for i in range(count):
                        of_block.append(values[:, i, :])
            if b == 0:
                nc.sync.dma_start(offsets[:], offs)

        for b in range(blocks):
            nc.vector.tensor_tensor(windows[b][:].indirect(offsets[:]), own_of_block[b], poi_of_block[b], ADD)
            nc.sync.dma_start(out_blocks[b], windows[b][:])
